import numpy as np
import ml_dtypes


def mxq(x, axis, fmt="e4m3"):
    dtype, down = {"e4m3": (ml_dtypes.float8_e4m3fn, 7), "e5m2": (ml_dtypes.float8_e5m2, 14)}[fmt]
    v = np.moveaxis(np.asarray(x, np.float32).astype(ml_dtypes.bfloat16).astype(np.float64), axis, -1)
    blocks = v.reshape(v.shape[:-1] + (-1, 32))
    amax = np.abs(blocks).max(-1, keepdims=True)
    byte = np.maximum(np.where(amax > 0, np.frexp(amax)[1] - 1 + 127, 0) - down, 1)
    scale = np.exp2(byte - 127.0)
    codes = (blocks / scale).astype(np.float32).astype(dtype).astype(np.float64)
    return np.moveaxis((codes * scale).reshape(v.shape), -1, axis)


WIDE = False


def mx_kscale(k):
    if not WIDE:
        return np.ones(k)
    levels = np.array([10, -10, 5, -5, 0])
    a = np.random.permutation(np.resize(levels, k // 512 * 4)).reshape(k // 512, 4)
    idx = np.arange(k)
    return np.exp2(a[idx // 512, idx % 128 // 32])


BF16 = ml_dtypes.bfloat16


def bf(x):
    return np.asarray(x, np.float32).astype(BF16)


def f64(x):
    return np.asarray(x).astype(np.float64)


E2M1 = np.array([0.0, 0.5, 1.0, 1.5, 2.0, 3.0, 4.0, 6.0, -0.0, -0.5, -1.0, -1.5, -2.0, -3.0, -4.0, -6.0])


def pack_weight(w, fmt):
    k, n = w.shape
    w = f64(bf(w)).reshape(k // 32, 32, n)
    amax = np.abs(w).max(1)
    if fmt == "e4m3":
        byte = np.frexp(amax)[1] - 1 + 127 - 7
    else:
        mant, ex = np.frexp(amax / 6.0)
        byte = np.where(mant > 0.5, ex, ex - 1) + 127
    byte = np.clip(np.where(amax > 0, byte, 1), 1, 254)
    scaled = (w * np.exp2(127.0 - byte)[:, None, :]).reshape(k, n).astype(np.float32)
    by_word = np.ascontiguousarray(scaled.reshape(k // 512, 128, 4, n).transpose(0, 1, 3, 2))
    if fmt == "e4m3":
        words = by_word.astype(ml_dtypes.float8_e4m3fn).view(np.uint8)
    else:
        c = by_word.astype(ml_dtypes.float4_e2m1fn).view(np.uint8) & 0xF
        words = c[..., 0::2] | (c[..., 1::2] << 4)
    return np.ascontiguousarray(words), np.ascontiguousarray(byte.astype(np.uint8).reshape(k // 512, 16, n))


def unpack_weight(words, scales, fmt):
    g, p, n, _ = words.shape
    if fmt == "e4m3":
        vals = np.ascontiguousarray(words).view(ml_dtypes.float8_e4m3fn).astype(np.float64)
    else:
        nib = np.empty((g, p, n, 4), np.uint8)
        nib[..., 0::2] = words & 0xF
        nib[..., 1::2] = words >> 4
        vals = E2M1[nib]
    vals = vals * np.repeat(np.exp2(scales.astype(np.float64) - 127.0), 8, axis=1)[..., None]
    return vals.transpose(0, 1, 3, 2).reshape(g * 512, n)

def pack4(w):
    words, scales = pack_weight(w, "e2m1")
    return words.reshape(words.shape[0], 128, -1), scales


def unpack4(words, scales):
    return unpack_weight(words.reshape(words.shape[0], 128, -1, 2), scales, "e2m1")


B, I, H = 1024, 1024, 1024
EPS = 1e-5


def ln(v):
    mu = v.mean(-1, keepdims=True)
    var = np.square(v - mu).mean(-1, keepdims=True)
    return (v - mu) / np.sqrt(var + EPS)


def sigmoid(v):
    return 1.0 / (1.0 + np.exp(-v))


def setup_inputs():
    s = mx_kscale(I)
    x = bf(np.random.standard_normal((B, I)) * s)
    h = bf(np.random.standard_normal((B, H)))
    r = bf(sigmoid(np.sqrt(2.0) * np.random.standard_normal((B, H))))
    z = bf(sigmoid(np.sqrt(2.0) * np.random.standard_normal((B, H))))
    W_in = np.random.standard_normal((H, I)) / np.sqrt(I) / s
    b_in = bf(np.random.standard_normal(H) * 0.5)
    W_hn = np.random.standard_normal((H, H)) / np.sqrt(H)
    b_hn = bf(np.random.standard_normal(H) * 0.5)
    W_in_words, W_in_scales = pack4(np.ascontiguousarray(W_in.T))
    W_hn_words, W_hn_scales = pack4(np.ascontiguousarray(W_hn.T))
    return {"x": x,
            "h": h,
            "r": r,
            "z": z,
            "W_in_words": W_in_words,
            "W_in_scales": W_in_scales,
            "b_in": b_in,
            "W_hn_words": W_hn_words,
            "W_hn_scales": W_hn_scales,
            "b_hn": b_hn}


def reference(x, h, r, z, W_in_words, W_in_scales, b_in, W_hn_words, W_hn_scales, b_hn):
    h = f64(h)
    r, z = f64(r), f64(z)
    i_n = ln((mxq(f64(x), 1, "e4m3") @ unpack4(W_in_words, W_in_scales)) + f64(b_in))
    h_n = ln((mxq(h, 1, "e4m3") @ unpack4(W_hn_words, W_hn_scales)) + f64(b_hn))
    n = np.tanh(i_n + r * h_n)
    return (1.0 - z) * n + z * h

@@ -1,0 +1,282 @@
+from contextlib import ExitStack
+
+import concourse.mybir as mybir
+from concourse.masks import make_identity
+
+F32 = mybir.dt.float32
+BF16 = mybir.dt.bfloat16
+I32 = mybir.dt.int32
+U32 = mybir.dt.uint32
+U8 = mybir.dt.uint8
+FP8X4 = mybir.dt.float8_e4m3fn_x4
+FP4X4 = mybir.dt.float4_e2m1fn_x4
+ALU = mybir.AluOpType
+ACT = mybir.ActivationFunctionType
+
+P = 128
+PACK = 4
+K_PASS = P * PACK
+BATCH, K, H = 1024, 1024, 1024
+ROW_TILES = BATCH // P
+PASSES = K // K_PASS
+BANK = 512
+HALVES = H // BANK
+EPS = 1e-5
+HN, IN = 0, 1
+LEAD = 3
+
+FLOPS = 2 * 2 * BATCH * K * H
+
+
+def tile_layernormgrucell_pb_kernel(
+    tc, x, h, r, z, W_in_words, W_in_scales, b_in, W_hn_words, W_hn_scales, b_hn, out
+):
+    nc = tc.nc
+    with ExitStack() as ctx:
+        const = ctx.enter_context(tc.tile_pool(name="const", bufs=1))
+        inputs = ctx.enter_context(tc.tile_pool(name="inputs", bufs=1))
+        stage = ctx.enter_context(tc.tile_pool(name="stage", bufs=2))
+        packed = ctx.enter_context(tc.tile_pool(name="packed", bufs=3))
+        work = ctx.enter_context(tc.tile_pool(name="work", bufs=3))
+        stats = ctx.enter_context(tc.tile_pool(name="stats", bufs=4))
+        flipped = ctx.enter_context(tc.psum_pool(name="flipped", bufs=4))
+        products = ctx.enter_context(tc.psum_pool(name="products", bufs=4))
+        ctx.enter_context(tc.manual_schedule())
+
+        w_words, w_plane = [], []
+        for path in (HN, IN):
+            w_words.append(const.tile([P, PASSES, 2 * H], U8, name="w_words%d" % path, align_bytes=64))
+            w_plane.append(const.tile([P, PASSES, H], U8, name="w_plane%d" % path, align_bytes=64))
+            nc.vector.memset(w_plane[path][:].bitcast(I32), 0)
+        ident = const.tile([P, P], F32)
+        make_identity(nc, ident[:])
+        minus_half = const.tile([P, 2], F32)
+        nc.gpsimd.memset(minus_half[:], -0.5)
+        bias = const.tile([P, 2, H], BF16)
+
+        h_sb, x_sb, r_sb, z_sb = [], [], [], []
+
+        def load_rows(loaded, src, label):
+            j = len(loaded)
+            rows = inputs.tile([P, K], BF16, name="%s%d" % (label, j))
+            nc.sync.dma_start(out=rows[:], in_=src[j * P : (j + 1) * P, :])
+            loaded.append(rows)
+
+        def load_weight(path, words, scales, b):
+            for quad in range(4):
+                nc.sync.dma_start(
+                    out=w_plane[path][32 * quad : 32 * quad + 4, :, :].bitcast(I32),
+                    in_=scales[:, 4 * quad : 4 * quad + 4, :].bitcast(I32).rearrange("g q n -> q g n"),
+                )
+            nc.sync.dma_start(
+                out=w_words[path][:].bitcast(I32),
+                in_=words.bitcast(I32).rearrange("g p c -> p g c"),
+            )
+            nc.sync.dma_start(out=bias[:, path, :], in_=b.partition_broadcast(P))
+
+        load_rows(h_sb, h, "h")
+        load_rows(x_sb, x, "x")
+        load_weight(HN, W_hn_words, W_hn_scales, b_hn)
+        load_weight(IN, W_in_words, W_in_scales, b_in)
+        for j in range(1, LEAD):
+            load_rows(h_sb, h, "h")
+            load_rows(x_sb, x, "x")
+        for j in range(ROW_TILES):
+            load_rows(r_sb, r, "r")
+            load_rows(z_sb, z, "z")
+            if j + LEAD < ROW_TILES:
+                load_rows(h_sb, h, "h")
+                load_rows(x_sb, x, "x")
+
+        kept = {}
+
+        def transpose(j):
+            grouped = stage.tile([P, 2, PASSES, P, PACK], BF16, align_bytes=64)
+            for path, rows in ((HN, h_sb[j]), (IN, x_sb[j])):
+                pairs = rows[:].bitcast(F32)
+                turned = flipped.tile([P, PASSES, 2, P], F32)
+                for g in range(PASSES):
+                    for u in range(2):
+                        nc.tensor.transpose(
+                            turned[:, g, u, :], pairs[:, 256 * g + u : 256 * (g + 1) : 2], ident[:]
+                        )
+                nc.scalar.copy(
+                    out=grouped[:, path].bitcast(F32),
+                    in_=turned[:].rearrange("p g u b -> p g b u"),
+                )
+            kept["grouped", j] = grouped
+
+        def quantise(j):
+            codes = packed.tile([P, 2, PASSES, P], U32, align_bytes=64)
+            plane = packed.tile([P, 2, PASSES, P], U8, align_bytes=64)
+            nc.vector.quantize_mx(
+                out=codes[:].rearrange("p a g b -> p (a g b)").bitcast(FP8X4),
+                scales=plane[:].rearrange("p a g b -> p (a g b)"),
+                in_=kept["grouped", j][:].rearrange("p a g b t -> p (a g b t)"),
+            )
+            kept["codes", j] = codes
+            kept["plane", j] = plane
+
+        def multiply(j):
+            codes, plane = kept["codes", j], kept["plane", j]
+            for path in (HN, IN):
+                for half in range(HALVES):
+                    acc = products.tile([P, BANK], F32)
+                    for g in range(PASSES):
+                        nc.tensor.matmul_mx(
+                            out=acc[:],
+                            lhsT=codes[:, path, g, :].bitcast(FP8X4),
+                            lhsT_scale=plane[:, path, g, :],
+                            rhs=w_words[path][:, g, 2 * BANK * half : 2 * BANK * (half + 1)].bitcast(FP4X4),
+                            rhs_scale=w_plane[path][:, g, BANK * half : BANK * (half + 1)],
+                            start=(g == 0),
+                            stop=(g == PASSES - 1),
+                        )
+                    kept["acc", j, path, half] = acc
+
+        def add_bias(j):
+            u = work.tile([P, 2, H], F32)
+            half_sums = stats.tile([P, 2, HALVES], F32)
+            for path in (HN, IN):
+                for half in range(HALVES):
+                    cols = slice(BANK * half, BANK * (half + 1))
+                    nc.vector.scalar_tensor_tensor(
+                        out=u[:, path, cols],
+                        in0=kept["acc", j, path, half][:],
+                        scalar=1.0,
+                        in1=bias[:, path, cols],
+                        op0=ALU.mult,
+                        op1=ALU.add,
+                        accum_out=half_sums[:, path, half : half + 1],
+                    )
+            kept["u", j] = u
+            kept["half_sums", j] = half_sums
+
+        def mean(j):
+            half_sums = kept["half_sums", j]
+            row_sums = stats.tile([P, 2], F32)
+            nc.gpsimd.tensor_tensor(out=row_sums[:], in0=half_sums[:, :, 0], in1=half_sums[:, :, 1], op=ALU.add)
+            minus_mean = stats.tile([P, 2], F32)
+            nc.gpsimd.tensor_scalar(
+                out=minus_mean[:], in0=row_sums[:], scalar1=-1.0 / H, scalar2=0.0, op0=ALU.mult, op1=ALU.add
+            )
+            kept["minus_mean", j] = minus_mean
+
+        def squares(j):
+            square_sums = stats.tile([P, 2], F32)
+            for path in (HN, IN):
+                unread = stage.tile([P, H], BF16)
+                nc.scalar.activation(
+                    out=unread[:],
+                    in_=kept["u", j][:, path, :],
+                    func=ACT.Square,
+                    bias=kept["minus_mean", j][:, path : path + 1],
+                    scale=1.0,
+                    accum_out=square_sums[:, path : path + 1],
+                )
+            kept["square_sums", j] = square_sums
+
+        def scalars(j):
+            var_eps = stats.tile([P, 2], F32)
+            nc.gpsimd.tensor_scalar(
+                out=var_eps[:], in0=kept["square_sums", j][:], scalar1=1.0 / H, scalar2=EPS, op0=ALU.mult, op1=ALU.add
+            )
+            rstd = stats.tile([P, 2], F32)
+            nc.gpsimd.tensor_tensor(out=rstd[:], in0=var_eps[:], in1=minus_half[:], op=ALU.pow)
+            ratio = stats.tile([P, 1], F32)
+            nc.gpsimd.tensor_scalar(
+                out=ratio[:],
+                in0=var_eps[:, IN : IN + 1],
+                scalar1=rstd[:, IN : IN + 1],
+                scalar2=rstd[:, HN : HN + 1],
+                op0=ALU.mult,
+                op1=ALU.mult,
+            )
+            shift = stats.tile([P, 1], F32)
+            nc.gpsimd.tensor_tensor(
+                out=shift[:], in0=kept["minus_mean", j][:, IN : IN + 1], in1=rstd[:, IN : IN + 1], op=ALU.mult
+            )
+            kept["rstd", j], kept["ratio", j], kept["shift", j] = rstd, ratio, shift
+
+        def reset_gate(j):
+            gated = work.tile([P, H], F32)
+            nc.vector.scalar_tensor_tensor(
+                out=gated[:],
+                in0=kept["u", j][:, HN, :],
+                scalar=kept["minus_mean", j][:, HN : HN + 1],
+                in1=r_sb[j][:],
+                op0=ALU.add,
+                op1=ALU.mult,
+            )
+            kept["gated", j] = gated
+
+        def add_input_path(j):
+            gated = kept["gated", j]
+            nc.vector.scalar_tensor_tensor(
+                out=gated[:],
+                in0=gated[:],
+                scalar=kept["ratio", j][:],
+                in1=kept["u", j][:, IN, :],
+                op0=ALU.mult,
+                op1=ALU.add,
+            )
+
+        def candidate(j):
+            n = work.tile([P, H], F32)
+            nc.scalar.activation(
+                out=n[:],
+                in_=kept["gated", j][:],
+                func=ACT.Tanh,
+                bias=kept["shift", j][:],
+                scale=kept["rstd", j][:, IN : IN + 1],
+            )
+            kept["n", j] = n
+
+        def keep_old(j):
+            blend = work.tile([P, H], F32)
+            nc.vector.tensor_tensor(out=blend[:], in0=z_sb[j][:], in1=h_sb[j][:], op=ALU.mult)
+            kept["blend", j] = blend
+
+        def take_new(j):
+            n = kept["n", j]
+            nc.vector.scalar_tensor_tensor(
+                out=n[:], in0=z_sb[j][:], scalar=1.0, in1=n[:], op0=ALU.subtract, op1=ALU.mult
+            )
+
+        def blend_and_store(j):
+            blend = kept["blend", j]
+            nc.vector.tensor_tensor(out=blend[:], in0=blend[:], in1=kept["n", j][:], op=ALU.subtract)
+            nc.sync.dma_start(out=out[j * P : (j + 1) * P, :], in_=blend[:])
+
+        def live(j):
+            return 0 <= j < ROW_TILES
+
+        transpose(0)
+        transpose(1)
+        quantise(0)
+        multiply(0)
+        quantise(1)
+        for i in range(ROW_TILES + 2):
+            if live(i + 2):
+                transpose(i + 2)
+            if live(i):
+                add_bias(i)
+                mean(i)
+                squares(i)
+            if live(i - 1):
+                reset_gate(i - 1)
+            if live(i - 2):
+                keep_old(i - 2)
+            if live(i - 1):
+                add_input_path(i - 1)
+                candidate(i - 1)
+            if live(i - 2):
+                take_new(i - 2)
+            if live(i + 2):
+                quantise(i + 2)
+            if live(i - 2):
+                blend_and_store(i - 2)
+            if live(i):
+                scalars(i)
+            if live(i + 1):
+                multiply(i + 1)

@@ -152,35 +152,35 @@ def tile_layernormgrucell_pb_kernel(
             kept["u", j] = u
             kept["half_sums", j] = half_sums
 
-        def mean(j):
-            half_sums = kept["half_sums", j]
-            row_sums = stats.tile([P, 2], F32)
-            nc.gpsimd.tensor_tensor(out=row_sums[:], in0=half_sums[:, :, 0], in1=half_sums[:, :, 1], op=ALU.add)
+        def deviations(j):
+            u, half_sums = kept["u", j], kept["half_sums", j]
             minus_mean = stats.tile([P, 2], F32)
-            nc.gpsimd.tensor_scalar(
-                out=minus_mean[:], in0=row_sums[:], scalar1=-1.0 / H, scalar2=0.0, op0=ALU.mult, op1=ALU.add
-            )
-            kept["minus_mean", j] = minus_mean
-
-        def squares(j):
             square_sums = stats.tile([P, 2], F32)
+            for path in (HN, IN):
+                unread_pair = stats.tile([P, HALVES], F32)
+                nc.scalar.activation(
+                    out=unread_pair[:],
+                    in_=half_sums[:, path, :],
+                    func=ACT.Identity,
+                    scale=-1.0 / H,
+                    accum_out=minus_mean[:, path : path + 1],
+                )
             for path in (HN, IN):
                 unread = stage.tile([P, H], BF16)
                 nc.scalar.activation(
                     out=unread[:],
-                    in_=kept["u", j][:, path, :],
+                    in_=u[:, path, :],
                     func=ACT.Square,
-                    bias=kept["minus_mean", j][:, path : path + 1],
+                    bias=minus_mean[:, path : path + 1],
                     scale=1.0,
                     accum_out=square_sums[:, path : path + 1],
                 )
-            kept["square_sums", j] = square_sums
-
-        def scalars(j):
             var_eps = stats.tile([P, 2], F32)
-            nc.gpsimd.tensor_scalar(
-                out=var_eps[:], in0=kept["square_sums", j][:], scalar1=1.0 / H, scalar2=EPS, op0=ALU.mult, op1=ALU.add
-            )
+            nc.scalar.activation(out=var_eps[:], in_=square_sums[:], func=ACT.Identity, bias=EPS, scale=1.0 / H)
+            kept["minus_mean", j], kept["var_eps", j] = minus_mean, var_eps
+
+        def inverse_std(j):
+            var_eps = kept["var_eps", j]
             rstd = stats.tile([P, 2], F32)
             nc.gpsimd.tensor_tensor(out=rstd[:], in0=var_eps[:], in1=minus_half[:], op=ALU.pow)
             ratio = stats.tile([P, 1], F32)
@@ -192,11 +192,7 @@ def tile_layernormgrucell_pb_kernel(
                 op0=ALU.mult,
                 op1=ALU.mult,
             )
-            shift = stats.tile([P, 1], F32)
-            nc.gpsimd.tensor_tensor(
-                out=shift[:], in0=kept["minus_mean", j][:, IN : IN + 1], in1=rstd[:, IN : IN + 1], op=ALU.mult
-            )
-            kept["rstd", j], kept["ratio", j], kept["shift", j] = rstd, ratio, shift
+            kept["rstd", j], kept["ratio", j] = rstd, ratio
 
         def reset_gate(j):
             gated = work.tile([P, H], F32)
@@ -222,14 +218,11 @@ def tile_layernormgrucell_pb_kernel(
             )
 
         def candidate(j):
+            rstd_i = kept["rstd", j][:, IN : IN + 1]
+            shift = stats.tile([P, 1], F32)
+            nc.scalar.activation(out=shift[:], in_=kept["minus_mean", j][:, IN : IN + 1], func=ACT.Copy, scale=rstd_i)
             n = work.tile([P, H], F32)
-            nc.scalar.activation(
-                out=n[:],
-                in_=kept["gated", j][:],
-                func=ACT.Tanh,
-                bias=kept["shift", j][:],
-                scale=kept["rstd", j][:, IN : IN + 1],
-            )
+            nc.scalar.activation(out=n[:], in_=kept["gated", j][:], func=ACT.Tanh, bias=shift[:], scale=rstd_i)
             kept["n", j] = n
 
         def keep_old(j):
@@ -261,8 +254,7 @@ def tile_layernormgrucell_pb_kernel(
                 transpose(i + 2)
             if live(i):
                 add_bias(i)
-                mean(i)
-                squares(i)
+                deviations(i)
             if live(i - 1):
                 reset_gate(i - 1)
             if live(i - 2):
@@ -277,6 +269,6 @@ def tile_layernormgrucell_pb_kernel(
             if live(i - 2):
                 blend_and_store(i - 2)
             if live(i):
-                scalars(i)
+                inverse_std(i)
             if live(i + 1):
                 multiply(i + 1)

@@ -43,6 +43,10 @@ def tile_layernormgrucell_pb_kernel(
         products = ctx.enter_context(tc.psum_pool(name="products", bufs=4))
         ctx.enter_context(tc.manual_schedule())
 
+        bias_rows = const.tile([P, 2, H], BF16)
+        nc.vector.memset(bias_rows[:], 0.0)
+        ones = const.tile([P, P], BF16)
+        nc.vector.memset(ones[:], 1.0)
         w_words, w_plane = [], []
         for path in (HN, IN):
             w_words.append(const.tile([P, PASSES, 2 * H], U8, name="w_words%d" % path, align_bytes=64))
@@ -62,7 +66,7 @@ def tile_layernormgrucell_pb_kernel(
             nc.sync.dma_start(out=rows[:], in_=src[j * P : (j + 1) * P, :])
             loaded.append(rows)
 
-        def load_weight(path, words, scales, b):
+        def load_weight(path, words, scales):
             for quad in range(4):
                 nc.sync.dma_start(
                     out=w_plane[path][32 * quad : 32 * quad + 4, :, :].bitcast(I32),
@@ -72,12 +76,13 @@ def tile_layernormgrucell_pb_kernel(
                 out=w_words[path][:].bitcast(I32),
                 in_=words.bitcast(I32).rearrange("g p c -> p g c"),
             )
-            nc.sync.dma_start(out=bias[:, path, :], in_=b.partition_broadcast(P))
 
         load_rows(h_sb, h, "h")
         load_rows(x_sb, x, "x")
-        load_weight(HN, W_hn_words, W_hn_scales, b_hn)
-        load_weight(IN, W_in_words, W_in_scales, b_in)
+        nc.sync.dma_start(out=bias_rows[0:1, HN, :], in_=b_hn.rearrange("(o n) -> o n", o=1))
+        nc.sync.dma_start(out=bias_rows[0:1, IN, :], in_=b_in.rearrange("(o n) -> o n", o=1))
+        load_weight(HN, W_hn_words, W_hn_scales)
+        load_weight(IN, W_in_words, W_in_scales)
         for j in range(1, LEAD):
             load_rows(h_sb, h, "h")
             load_rows(x_sb, x, "x")
@@ -89,6 +94,14 @@ def tile_layernormgrucell_pb_kernel(
                 load_rows(x_sb, x, "x")
 
         kept = {}
+
+        def spread_bias():
+            for path in (HN, IN):
+                for half in range(HALVES):
+                    cols = slice(BANK * half, BANK * (half + 1))
+                    spread = products.tile([P, BANK], F32, tag="acc")
+                    nc.tensor.matmul(out=spread[:], lhsT=ones[:], rhs=bias_rows[:, path, cols], start=True, stop=True)
+                    nc.vector.tensor_copy(out=bias[:, path, cols], in_=spread[:])
 
         def transpose(j):
             grouped = stage.tile([P, 2, PASSES, P, PACK], BF16, align_bytes=64)
@@ -245,9 +258,10 @@ def tile_layernormgrucell_pb_kernel(
             return 0 <= j < ROW_TILES
 
         transpose(0)
-        transpose(1)
         quantise(0)
+        spread_bias()
         multiply(0)
+        transpose(1)
         quantise(1)
         for i in range(ROW_TILES + 2):
             if live(i + 2):

@@ -39,7 +39,9 @@ def tile_layernormgrucell_pb_kernel(
         packed = ctx.enter_context(tc.tile_pool(name="packed", bufs=3))
         work = ctx.enter_context(tc.tile_pool(name="work", bufs=3))
         stats = ctx.enter_context(tc.tile_pool(name="stats", bufs=4))
-        flipped = ctx.enter_context(tc.psum_pool(name="flipped", bufs=4))
+        blends = ctx.enter_context(tc.tile_pool(name="blends", bufs=4))
+        flipped = ctx.enter_context(tc.psum_pool(name="flipped", bufs=2))
+        gates = ctx.enter_context(tc.psum_pool(name="gates", bufs=2))
         products = ctx.enter_context(tc.psum_pool(name="products", bufs=4))
         ctx.enter_context(tc.manual_schedule())
 
@@ -54,6 +56,8 @@ def tile_layernormgrucell_pb_kernel(
             nc.vector.memset(w_plane[path][:].bitcast(I32), 0)
         ident = const.tile([P, P], F32)
         make_identity(nc, ident[:])
+        ident_bf = const.tile([P, P], BF16)
+        make_identity(nc, ident_bf[:])
         minus_half = const.tile([P, 2], F32)
         nc.gpsimd.memset(minus_half[:], -0.5)
         bias = const.tile([P, 2, H], BF16)
@@ -207,16 +211,26 @@ def tile_layernormgrucell_pb_kernel(
             )
             kept["rstd", j], kept["ratio", j] = rstd, ratio
 
+        def reset_to_psum(j):
+            for half in range(HALVES):
+                r_bank = gates.tile([P, BANK], F32)
+                nc.tensor.matmul(
+                    out=r_bank[:], lhsT=ident_bf[:], rhs=r_sb[j][:, BANK * half : BANK * (half + 1)], start=True, stop=True
+                )
+                kept["r_bank", j, half] = r_bank
+
         def reset_gate(j):
             gated = work.tile([P, H], F32)
-            nc.vector.scalar_tensor_tensor(
-                out=gated[:],
-                in0=kept["u", j][:, HN, :],
-                scalar=kept["minus_mean", j][:, HN : HN + 1],
-                in1=r_sb[j][:],
-                op0=ALU.add,
-                op1=ALU.mult,
-            )
+            for half in range(HALVES):
+                cols = slice(BANK * half, BANK * (half + 1))
+                nc.vector.scalar_tensor_tensor(
+                    out=gated[:, cols],
+                    in0=kept["u", j][:, HN, cols],
+                    scalar=kept["minus_mean", j][:, HN : HN + 1],
+                    in1=kept["r_bank", j, half][:],
+                    op0=ALU.add,
+                    op1=ALU.mult,
+                )
             kept["gated", j] = gated
 
         def add_input_path(j):
@@ -239,8 +253,8 @@ def tile_layernormgrucell_pb_kernel(
             kept["n", j] = n
 
         def keep_old(j):
-            blend = work.tile([P, H], F32)
-            nc.vector.tensor_tensor(out=blend[:], in0=z_sb[j][:], in1=h_sb[j][:], op=ALU.mult)
+            blend = blends.tile([P, H], F32)
+            nc.gpsimd.tensor_tensor(out=blend[:], in0=z_sb[j][:], in1=h_sb[j][:], op=ALU.mult)
             kept["blend", j] = blend
 
         def take_new(j):
@@ -263,16 +277,16 @@ def tile_layernormgrucell_pb_kernel(
         multiply(0)
         transpose(1)
         quantise(1)
+        keep_old(0)
         for i in range(ROW_TILES + 2):
             if live(i + 2):
                 transpose(i + 2)
-            if live(i):
-                add_bias(i)
-                deviations(i)
             if live(i - 1):
                 reset_gate(i - 1)
-            if live(i - 2):
-                keep_old(i - 2)
+            if live(i):
+                reset_to_psum(i)
+                add_bias(i)
+                deviations(i)
             if live(i - 1):
                 add_input_path(i - 1)
                 candidate(i - 1)
@@ -285,4 +299,5 @@ def tile_layernormgrucell_pb_kernel(
             if live(i):
                 inverse_std(i)
             if live(i + 1):
+                keep_old(i + 1)
                 multiply(i + 1)

@@ -197,19 +197,19 @@ def tile_layernormgrucell_pb_kernel(
             kept["minus_mean", j], kept["var_eps", j] = minus_mean, var_eps
 
         def inverse_std(j):
-            var_eps = kept["var_eps", j]
             rstd = stats.tile([P, 2], F32)
-            nc.gpsimd.tensor_tensor(out=rstd[:], in0=var_eps[:], in1=minus_half[:], op=ALU.pow)
+            nc.gpsimd.tensor_tensor(out=rstd[:], in0=kept["var_eps", j][:], in1=minus_half[:], op=ALU.pow)
+            kept["rstd", j] = rstd
+
+        def row_scalars(j):
+            rstd_h, rstd_i = kept["rstd", j][:, HN : HN + 1], kept["rstd", j][:, IN : IN + 1]
+            std_i = stats.tile([P, 1], F32)
+            nc.scalar.activation(out=std_i[:], in_=kept["var_eps", j][:, IN : IN + 1], func=ACT.Copy, scale=rstd_i)
+            shift = stats.tile([P, 1], F32)
+            nc.scalar.activation(out=shift[:], in_=kept["minus_mean", j][:, IN : IN + 1], func=ACT.Copy, scale=rstd_i)
             ratio = stats.tile([P, 1], F32)
-            nc.gpsimd.tensor_scalar(
-                out=ratio[:],
-                in0=var_eps[:, IN : IN + 1],
-                scalar1=rstd[:, IN : IN + 1],
-                scalar2=rstd[:, HN : HN + 1],
-                op0=ALU.mult,
-                op1=ALU.mult,
-            )
-            kept["rstd", j], kept["ratio", j] = rstd, ratio
+            nc.scalar.activation(out=ratio[:], in_=std_i[:], func=ACT.Copy, scale=rstd_h)
+            kept["ratio", j], kept["shift", j] = ratio, shift
 
         def reset_to_psum(j):
             for half in range(HALVES):
@@ -245,11 +245,14 @@ def tile_layernormgrucell_pb_kernel(
             )
 
         def candidate(j):
-            rstd_i = kept["rstd", j][:, IN : IN + 1]
-            shift = stats.tile([P, 1], F32)
-            nc.scalar.activation(out=shift[:], in_=kept["minus_mean", j][:, IN : IN + 1], func=ACT.Copy, scale=rstd_i)
             n = work.tile([P, H], F32)
-            nc.scalar.activation(out=n[:], in_=kept["gated", j][:], func=ACT.Tanh, bias=shift[:], scale=rstd_i)
+            nc.scalar.activation(
+                out=n[:],
+                in_=kept["gated", j][:],
+                func=ACT.Tanh,
+                bias=kept["shift", j][:],
+                scale=kept["rstd", j][:, IN : IN + 1],
+            )
             kept["n", j] = n
 
         def keep_old(j):
@@ -283,6 +286,7 @@ def tile_layernormgrucell_pb_kernel(
                 transpose(i + 2)
             if live(i - 1):
                 reset_gate(i - 1)
+                row_scalars(i - 1)
             if live(i):
                 reset_to_psum(i)
                 add_bias(i)

@@ -23,7 +23,8 @@ BANK = 512
 HALVES = H // BANK
 EPS = 1e-5
 HN, IN = 0, 1
-LEAD = 3
+LAST_PARTS = 2
+LEAD = 2
 
 FLOPS = 2 * 2 * BATCH * K * H
 
@@ -45,19 +46,20 @@ def tile_layernormgrucell_pb_kernel(
         products = ctx.enter_context(tc.psum_pool(name="products", bufs=4))
         ctx.enter_context(tc.manual_schedule())
 
-        bias_rows = const.tile([P, 2, H], BF16)
-        nc.vector.memset(bias_rows[:], 0.0)
-        ones = const.tile([P, P], BF16)
-        nc.vector.memset(ones[:], 1.0)
         w_words, w_plane = [], []
+        bias_rows = const.tile([P, 2, H], BF16)
         for path in (HN, IN):
             w_words.append(const.tile([P, PASSES, 2 * H], U8, name="w_words%d" % path, align_bytes=64))
             w_plane.append(const.tile([P, PASSES, H], U8, name="w_plane%d" % path, align_bytes=64))
-            nc.vector.memset(w_plane[path][:].bitcast(I32), 0)
+        nc.vector.memset(w_plane[HN][:].bitcast(I32), 0)
+        nc.vector.memset(bias_rows[:].bitcast(I32), 0)
+        nc.vector.memset(w_plane[IN][:].bitcast(I32), 0)
         ident = const.tile([P, P], F32)
         make_identity(nc, ident[:])
         ident_bf = const.tile([P, P], BF16)
         make_identity(nc, ident_bf[:])
+        ones = const.tile([P, P], BF16)
+        nc.gpsimd.memset(ones[:], 1.0)
         minus_half = const.tile([P, 2], F32)
         nc.gpsimd.memset(minus_half[:], -0.5)
         bias = const.tile([P, 2, H], BF16)
@@ -70,12 +72,14 @@ def tile_layernormgrucell_pb_kernel(
             nc.sync.dma_start(out=rows[:], in_=src[j * P : (j + 1) * P, :])
             loaded.append(rows)
 
-        def load_weight(path, words, scales):
+        def load_scales(path, scales):
             for quad in range(4):
                 nc.sync.dma_start(
                     out=w_plane[path][32 * quad : 32 * quad + 4, :, :].bitcast(I32),
                     in_=scales[:, 4 * quad : 4 * quad + 4, :].bitcast(I32).rearrange("g q n -> q g n"),
                 )
+
+        def load_words(path, words):
             nc.sync.dma_start(
                 out=w_words[path][:].bitcast(I32),
                 in_=words.bitcast(I32).rearrange("g p c -> p g c"),
@@ -83,34 +87,36 @@ def tile_layernormgrucell_pb_kernel(
 
         load_rows(h_sb, h, "h")
         load_rows(x_sb, x, "x")
+        load_scales(HN, W_hn_scales)
         nc.sync.dma_start(out=bias_rows[0:1, HN, :], in_=b_hn.rearrange("(o n) -> o n", o=1))
         nc.sync.dma_start(out=bias_rows[0:1, IN, :], in_=b_in.rearrange("(o n) -> o n", o=1))
-        load_weight(HN, W_hn_words, W_hn_scales)
-        load_weight(IN, W_in_words, W_in_scales)
-        for j in range(1, LEAD):
-            load_rows(h_sb, h, "h")
-            load_rows(x_sb, x, "x")
+        load_words(HN, W_hn_words)
+        load_scales(IN, W_in_scales)
+        load_words(IN, W_in_words)
         for j in range(ROW_TILES):
-            load_rows(r_sb, r, "r")
+            for ahead in range(LEAD if j == 0 else 1):
+                if len(h_sb) < ROW_TILES:
+                    load_rows(h_sb, h, "h")
+                    load_rows(x_sb, x, "x")
+                if ahead == 0:
+                    load_rows(r_sb, r, "r")
             load_rows(z_sb, z, "z")
-            if j + LEAD < ROW_TILES:
-                load_rows(h_sb, h, "h")
-                load_rows(x_sb, x, "x")
 
         kept = {}
 
-        def spread_bias():
-            for path in (HN, IN):
-                for half in range(HALVES):
-                    cols = slice(BANK * half, BANK * (half + 1))
-                    spread = products.tile([P, BANK], F32, tag="acc")
-                    nc.tensor.matmul(out=spread[:], lhsT=ones[:], rhs=bias_rows[:, path, cols], start=True, stop=True)
-                    nc.vector.tensor_copy(out=bias[:, path, cols], in_=spread[:])
+        def spread_bias(path, pool, tag, copy):
+            for half in range(HALVES):
+                cols = slice(BANK * half, BANK * (half + 1))
+                spread = pool.tile([P, BANK], F32, tag=tag)
+                nc.tensor.matmul(out=spread[:], lhsT=ones[:], rhs=bias_rows[:, path, cols], start=True, stop=True)
+                copy(out=bias[:, path, cols], in_=spread[:])
 
-        def transpose(j):
-            grouped = stage.tile([P, 2, PASSES, P, PACK], BF16, align_bytes=64)
-            for path, rows in ((HN, h_sb[j]), (IN, x_sb[j])):
-                pairs = rows[:].bitcast(F32)
+        def transpose(j, paths=(HN, IN)):
+            if paths[0] == HN:
+                kept["grouped", j] = stage.tile([P, 2, PASSES, P, PACK], BF16, align_bytes=64, name="grouped")
+            grouped = kept["grouped", j]
+            for path in paths:
+                pairs = (h_sb, x_sb)[path][j][:].bitcast(F32)
                 turned = flipped.tile([P, PASSES, 2, P], F32)
                 for g in range(PASSES):
                     for u in range(2):
@@ -121,24 +127,23 @@ def tile_layernormgrucell_pb_kernel(
                     out=grouped[:, path].bitcast(F32),
                     in_=turned[:].rearrange("p g u b -> p g b u"),
                 )
-            kept["grouped", j] = grouped
 
-        def quantise(j):
-            codes = packed.tile([P, 2, PASSES, P], U32, align_bytes=64)
-            plane = packed.tile([P, 2, PASSES, P], U8, align_bytes=64)
+        def quantise(j, paths=(HN, IN)):
+            if paths[0] == HN:
+                kept["codes", j] = packed.tile([P, 2, PASSES, P], U32, align_bytes=64, name="codes")
+                kept["plane", j] = packed.tile([P, 2, PASSES, P], U8, align_bytes=64, name="plane")
+            some = slice(paths[0], paths[-1] + 1)
             nc.vector.quantize_mx(
-                out=codes[:].rearrange("p a g b -> p (a g b)").bitcast(FP8X4),
-                scales=plane[:].rearrange("p a g b -> p (a g b)"),
-                in_=kept["grouped", j][:].rearrange("p a g b t -> p (a g b t)"),
+                out=kept["codes", j][:, some].rearrange("p a g b -> p (a g b)").bitcast(FP8X4),
+                scales=kept["plane", j][:, some].rearrange("p a g b -> p (a g b)"),
+                in_=kept["grouped", j][:, some].rearrange("p a g b t -> p (a g b t)"),
             )
-            kept["codes", j] = codes
-            kept["plane", j] = plane
 
-        def multiply(j):
+        def multiply(j, paths=(HN, IN)):
             codes, plane = kept["codes", j], kept["plane", j]
-            for path in (HN, IN):
+            for path in paths:
                 for half in range(HALVES):
-                    acc = products.tile([P, BANK], F32)
+                    acc = products.tile([P, BANK], F32, tag="acc")
                     for g in range(PASSES):
                         nc.tensor.matmul_mx(
                             out=acc[:],
@@ -182,7 +187,6 @@ def tile_layernormgrucell_pb_kernel(
                     scale=-1.0 / H,
                     accum_out=minus_mean[:, path : path + 1],
                 )
-            for path in (HN, IN):
                 unread = stage.tile([P, H], BF16)
                 nc.scalar.activation(
                     out=unread[:],
@@ -213,7 +217,7 @@ def tile_layernormgrucell_pb_kernel(
 
         def reset_to_psum(j):
             for half in range(HALVES):
-                r_bank = gates.tile([P, BANK], F32)
+                r_bank = gates.tile([P, BANK], F32, tag="r_bank")
                 nc.tensor.matmul(
                     out=r_bank[:], lhsT=ident_bf[:], rhs=r_sb[j][:, BANK * half : BANK * (half + 1)], start=True, stop=True
                 )
@@ -233,26 +237,32 @@ def tile_layernormgrucell_pb_kernel(
                 )
             kept["gated", j] = gated
 
+        def column_parts(j):
+            parts = LAST_PARTS if j == ROW_TILES - 1 else 1
+            return [slice(c * H // parts, (c + 1) * H // parts) for c in range(parts)]
+
         def add_input_path(j):
             gated = kept["gated", j]
-            nc.vector.scalar_tensor_tensor(
-                out=gated[:],
-                in0=gated[:],
-                scalar=kept["ratio", j][:],
-                in1=kept["u", j][:, IN, :],
-                op0=ALU.mult,
-                op1=ALU.add,
-            )
+            for cols in column_parts(j):
+                nc.vector.scalar_tensor_tensor(
+                    out=gated[:, cols],
+                    in0=gated[:, cols],
+                    scalar=kept["ratio", j][:],
+                    in1=kept["u", j][:, IN, cols],
+                    op0=ALU.mult,
+                    op1=ALU.add,
+                )
 
         def candidate(j):
             n = work.tile([P, H], F32)
-            nc.scalar.activation(
-                out=n[:],
-                in_=kept["gated", j][:],
-                func=ACT.Tanh,
-                bias=kept["shift", j][:],
-                scale=kept["rstd", j][:, IN : IN + 1],
-            )
+            for cols in column_parts(j):
+                nc.scalar.activation(
+                    out=n[:, cols],
+                    in_=kept["gated", j][:, cols],
+                    func=ACT.Tanh,
+                    bias=kept["shift", j][:],
+                    scale=kept["rstd", j][:, IN : IN + 1],
+                )
             kept["n", j] = n
 
         def keep_old(j):
@@ -262,26 +272,38 @@ def tile_layernormgrucell_pb_kernel(
 
         def take_new(j):
             n = kept["n", j]
-            nc.vector.scalar_tensor_tensor(
-                out=n[:], in0=z_sb[j][:], scalar=1.0, in1=n[:], op0=ALU.subtract, op1=ALU.mult
-            )
+            for cols in column_parts(j):
+                nc.vector.scalar_tensor_tensor(
+                    out=n[:, cols], in0=z_sb[j][:, cols], scalar=1.0, in1=n[:, cols], op0=ALU.subtract, op1=ALU.mult
+                )
 
         def blend_and_store(j):
-            blend = kept["blend", j]
-            nc.vector.tensor_tensor(out=blend[:], in0=blend[:], in1=kept["n", j][:], op=ALU.subtract)
-            nc.sync.dma_start(out=out[j * P : (j + 1) * P, :], in_=blend[:])
+            blend, n = kept["blend", j], kept["n", j]
+            for cols in column_parts(j):
+                nc.vector.tensor_tensor(out=blend[:, cols], in0=blend[:, cols], in1=n[:, cols], op=ALU.subtract)
+                nc.sync.dma_start(out=out[j * P : (j + 1) * P, cols], in_=blend[:, cols])
 
         def live(j):
             return 0 <= j < ROW_TILES
 
-        transpose(0)
-        quantise(0)
-        spread_bias()
+        transpose(0, (HN,))
+        quantise(0, (HN,))
+        transpose(0, (IN,))
+        quantise(0, (IN,))
+        spread_bias(HN, gates, "r_bank", nc.scalar.copy)
+        spread_bias(IN, products, "acc", nc.vector.tensor_copy)
         multiply(0)
         transpose(1)
+        add_bias(0)
         quantise(1)
+        deviations(0)
+        reset_to_psum(0)
+        multiply(1)
+        transpose(2)
+        inverse_std(0)
         keep_old(0)
-        for i in range(ROW_TILES + 2):
+        keep_old(1)
+        for i in range(1, ROW_TILES + 2):
             if live(i + 2):
                 transpose(i + 2)
             if live(i - 1):
@@ -290,14 +312,15 @@ def tile_layernormgrucell_pb_kernel(
             if live(i):
                 reset_to_psum(i)
                 add_bias(i)
+            if live(i + 1):
+                quantise(i + 1)
+            if live(i):
                 deviations(i)
+            if live(i - 2):
+                take_new(i - 2)
             if live(i - 1):
                 add_input_path(i - 1)
                 candidate(i - 1)
-            if live(i - 2):
-                take_new(i - 2)
-            if live(i + 2):
-                quantise(i + 2)
             if live(i - 2):
                 blend_and_store(i - 2)
             if live(i):

@@ -40,7 +40,7 @@ def tile_layernormgrucell_pb_kernel(
         packed = ctx.enter_context(tc.tile_pool(name="packed", bufs=3))
         work = ctx.enter_context(tc.tile_pool(name="work", bufs=3))
         stats = ctx.enter_context(tc.tile_pool(name="stats", bufs=4))
-        blends = ctx.enter_context(tc.tile_pool(name="blends", bufs=4))
+        blends = ctx.enter_context(tc.tile_pool(name="blends", bufs=3))
         flipped = ctx.enter_context(tc.psum_pool(name="flipped", bufs=2))
         gates = ctx.enter_context(tc.psum_pool(name="gates", bufs=2))
         products = ctx.enter_context(tc.psum_pool(name="products", bufs=4))
@@ -266,9 +266,9 @@ def tile_layernormgrucell_pb_kernel(
             kept["n", j] = n
 
         def keep_old(j):
-            blend = blends.tile([P, H], F32)
-            nc.gpsimd.tensor_tensor(out=blend[:], in0=z_sb[j][:], in1=h_sb[j][:], op=ALU.mult)
-            kept["blend", j] = blend
+            old = blends.tile([P, H], F32)
+            nc.gpsimd.tensor_tensor(out=old[:], in0=z_sb[j][:], in1=h_sb[j][:], op=ALU.mult)
+            kept["old", j] = old
 
         def take_new(j):
             n = kept["n", j]
@@ -278,10 +278,10 @@ def tile_layernormgrucell_pb_kernel(
                 )
 
         def blend_and_store(j):
-            blend, n = kept["blend", j], kept["n", j]
+            old, n = kept["old", j], kept["n", j]
             for cols in column_parts(j):
-                nc.vector.tensor_tensor(out=blend[:, cols], in0=blend[:, cols], in1=n[:, cols], op=ALU.subtract)
-                nc.sync.dma_start(out=out[j * P : (j + 1) * P, cols], in_=blend[:, cols])
+                nc.vector.tensor_tensor(out=n[:, cols], in0=old[:, cols], in1=n[:, cols], op=ALU.subtract)
+                nc.sync.dma_start(out=out[j * P : (j + 1) * P, cols], in_=n[:, cols])
 
         def live(j):
             return 0 <= j < ROW_TILES
@@ -302,13 +302,15 @@ def tile_layernormgrucell_pb_kernel(
         transpose(2)
         inverse_std(0)
         keep_old(0)
-        keep_old(1)
         for i in range(1, ROW_TILES + 2):
+            if live(i):
+                keep_old(i)
+            if live(i - 1) and i > 1:
+                inverse_std(i - 1)
             if live(i + 2):
                 transpose(i + 2)
             if live(i - 1):
                 reset_gate(i - 1)
-                row_scalars(i - 1)
             if live(i):
                 reset_to_psum(i)
                 add_bias(i)
@@ -319,12 +321,10 @@ def tile_layernormgrucell_pb_kernel(
             if live(i - 2):
                 take_new(i - 2)
             if live(i - 1):
+                row_scalars(i - 1)
                 add_input_path(i - 1)
                 candidate(i - 1)
             if live(i - 2):
                 blend_and_store(i - 2)
-            if live(i):
-                inverse_std(i)
             if live(i + 1):
-                keep_old(i + 1)
                 multiply(i + 1)

@@ -305,12 +305,11 @@ def tile_layernormgrucell_pb_kernel(
         for i in range(1, ROW_TILES + 2):
             if live(i):
                 keep_old(i)
-            if live(i - 1) and i > 1:
-                inverse_std(i - 1)
-            if live(i + 2):
-                transpose(i + 2)
             if live(i - 1):
                 reset_gate(i - 1)
+                row_scalars(i - 1)
+            if live(i + 2):
+                transpose(i + 2)
             if live(i):
                 reset_to_psum(i)
                 add_bias(i)
@@ -321,10 +320,11 @@ def tile_layernormgrucell_pb_kernel(
             if live(i - 2):
                 take_new(i - 2)
             if live(i - 1):
-                row_scalars(i - 1)
                 add_input_path(i - 1)
                 candidate(i - 1)
             if live(i - 2):
                 blend_and_store(i - 2)
+            if live(i):
+                inverse_std(i)
             if live(i + 1):
                 multiply(i + 1)

@@ -23,6 +23,7 @@ BANK = 512
 HALVES = H // BANK
 EPS = 1e-5
 HN, IN = 0, 1
+POOL_COLS = 512
 LAST_PARTS = 2
 LEAD = 2
 
@@ -40,7 +41,7 @@ def tile_layernormgrucell_pb_kernel(
         packed = ctx.enter_context(tc.tile_pool(name="packed", bufs=3))
         work = ctx.enter_context(tc.tile_pool(name="work", bufs=3))
         stats = ctx.enter_context(tc.tile_pool(name="stats", bufs=4))
-        blends = ctx.enter_context(tc.tile_pool(name="blends", bufs=3))
+        blends = ctx.enter_context(tc.tile_pool(name="blends", bufs=4))
         flipped = ctx.enter_context(tc.psum_pool(name="flipped", bufs=2))
         gates = ctx.enter_context(tc.psum_pool(name="gates", bufs=2))
         products = ctx.enter_context(tc.psum_pool(name="products", bufs=4))
@@ -254,7 +255,7 @@ def tile_layernormgrucell_pb_kernel(
                 )
 
         def candidate(j):
-            n = work.tile([P, H], F32)
+            n = blends.tile([P, H], F32)
             for cols in column_parts(j):
                 nc.scalar.activation(
                     out=n[:, cols],
@@ -277,11 +278,12 @@ def tile_layernormgrucell_pb_kernel(
                     out=n[:, cols], in0=z_sb[j][:, cols], scalar=1.0, in1=n[:, cols], op0=ALU.subtract, op1=ALU.mult
                 )
 
-        def blend_and_store(j):
+        def blend(j, engine, cols):
             old, n = kept["old", j], kept["n", j]
-            for cols in column_parts(j):
-                nc.vector.tensor_tensor(out=n[:, cols], in0=old[:, cols], in1=n[:, cols], op=ALU.subtract)
-                nc.sync.dma_start(out=out[j * P : (j + 1) * P, cols], in_=n[:, cols])
+            engine.tensor_tensor(out=n[:, cols], in0=old[:, cols], in1=n[:, cols], op=ALU.subtract)
+
+        def store(j, cols):
+            nc.sync.dma_start(out=out[j * P : (j + 1) * P, cols], in_=kept["n", j][:, cols])
 
         def live(j):
             return 0 <= j < ROW_TILES
@@ -302,7 +304,10 @@ def tile_layernormgrucell_pb_kernel(
         transpose(2)
         inverse_std(0)
         keep_old(0)
+        pool_cols, vector_cols = slice(0, POOL_COLS), slice(POOL_COLS, H)
         for i in range(1, ROW_TILES + 2):
+            if live(i - 3):
+                blend(i - 3, nc.gpsimd, pool_cols)
             if live(i):
                 keep_old(i)
             if live(i - 1):
@@ -317,14 +322,19 @@ def tile_layernormgrucell_pb_kernel(
                 quantise(i + 1)
             if live(i):
                 deviations(i)
-            if live(i - 2):
-                take_new(i - 2)
+            if live(i - 3):
+                blend(i - 3, nc.vector, vector_cols)
+                store(i - 3, pool_cols)
+                store(i - 3, vector_cols)
             if live(i - 1):
                 add_input_path(i - 1)
                 candidate(i - 1)
             if live(i - 2):
-                blend_and_store(i - 2)
+                take_new(i - 2)
             if live(i):
                 inverse_std(i)
             if live(i + 1):
                 multiply(i + 1)
+        for cols in column_parts(ROW_TILES - 1):
+            blend(ROW_TILES - 1, nc.vector, cols)
+            store(ROW_TILES - 1, cols)

@@ -21,6 +21,7 @@ ROW_TILES = BATCH // P
 PASSES = K // K_PASS
 BANK = 512
 HALVES = H // BANK
+WORD_BLOCKS = H * 2 // 4 // P
 EPS = 1e-5
 HN, IN = 0, 1
 POOL_COLS = 512
@@ -43,7 +44,7 @@ def tile_layernormgrucell_pb_kernel(
         stats = ctx.enter_context(tc.tile_pool(name="stats", bufs=4))
         blends = ctx.enter_context(tc.tile_pool(name="blends", bufs=4))
         flipped = ctx.enter_context(tc.psum_pool(name="flipped", bufs=2))
-        gates = ctx.enter_context(tc.psum_pool(name="gates", bufs=2))
+        gates = ctx.enter_context(tc.psum_pool(name="gates", bufs=1))
         products = ctx.enter_context(tc.psum_pool(name="products", bufs=4))
         ctx.enter_context(tc.manual_schedule())
 
@@ -105,9 +106,10 @@ def tile_layernormgrucell_pb_kernel(
 
         kept = {}
 
-        def spread_bias(path, pool, tag, copy):
+        def spread_bias(path, banks, copy):
             for half in range(HALVES):
                 cols = slice(BANK * half, BANK * (half + 1))
+                pool, tag = banks[half]
                 spread = pool.tile([P, BANK], F32, tag=tag)
                 nc.tensor.matmul(out=spread[:], lhsT=ones[:], rhs=bias_rows[:, path, cols], start=True, stop=True)
                 copy(out=bias[:, path, cols], in_=spread[:])
@@ -118,7 +120,7 @@ def tile_layernormgrucell_pb_kernel(
             grouped = kept["grouped", j]
             for path in paths:
                 pairs = (h_sb, x_sb)[path][j][:].bitcast(F32)
-                turned = flipped.tile([P, PASSES, 2, P], F32)
+                turned = flipped.tile([P, PASSES, 2, P], F32, tag="turned")
                 for g in range(PASSES):
                     for u in range(2):
                         nc.tensor.transpose(
@@ -217,26 +219,38 @@ def tile_layernormgrucell_pb_kernel(
             kept["ratio", j], kept["shift", j] = ratio, shift
 
         def reset_to_psum(j):
+            r_bank = gates.tile([P, H], BF16, tag="r_bank")
             for half in range(HALVES):
-                r_bank = gates.tile([P, BANK], F32, tag="r_bank")
-                nc.tensor.matmul(
-                    out=r_bank[:], lhsT=ident_bf[:], rhs=r_sb[j][:, BANK * half : BANK * (half + 1)], start=True, stop=True
-                )
-                kept["r_bank", j, half] = r_bank
+                cols = slice(BANK * half, BANK * (half + 1))
+                nc.tensor.matmul(out=r_bank[:, cols], lhsT=ident_bf[:], rhs=r_sb[j][:, cols], start=True, stop=True)
+            kept["r_bank", j] = r_bank
 
         def reset_gate(j):
             gated = work.tile([P, H], F32)
-            for half in range(HALVES):
-                cols = slice(BANK * half, BANK * (half + 1))
-                nc.vector.scalar_tensor_tensor(
-                    out=gated[:, cols],
-                    in0=kept["u", j][:, HN, cols],
-                    scalar=kept["minus_mean", j][:, HN : HN + 1],
-                    in1=kept["r_bank", j, half][:],
-                    op0=ALU.add,
-                    op1=ALU.mult,
-                )
+            nc.vector.scalar_tensor_tensor(
+                out=gated[:],
+                in0=kept["u", j][:, HN, :],
+                scalar=kept["minus_mean", j][:, HN : HN + 1],
+                in1=kept["r_bank", j][:],
+                op0=ALU.add,
+                op1=ALU.mult,
+            )
             kept["gated", j] = gated
+
+        def turn_update(j):
+            words = z_sb[j][:].bitcast(F32)
+            turned = flipped.tile([P, WORD_BLOCKS, P], F32, tag="turned")
+            for c in range(WORD_BLOCKS):
+                nc.tensor.transpose(turned[:, c, :], words[:, P * c : P * (c + 1)], ident[:])
+            z_turned = stage.tile([P, WORD_BLOCKS, P], F32)
+            nc.scalar.copy(out=z_turned[:], in_=turned[:])
+            kept["z_turned", j] = z_turned
+
+        def update_to_psum(j):
+            z_bank = gates.tile([P, WORD_BLOCKS * P], F32, tag="z_bank")
+            for c in range(WORD_BLOCKS):
+                nc.tensor.transpose(z_bank[:, P * c : P * (c + 1)], kept["z_turned", j][:, c, :], ident[:])
+            kept["z_bank", j] = z_bank
 
         def column_parts(j):
             parts = LAST_PARTS if j == ROW_TILES - 1 else 1
@@ -272,10 +286,10 @@ def tile_layernormgrucell_pb_kernel(
             kept["old", j] = old
 
         def take_new(j):
-            n = kept["n", j]
+            n, z_bank = kept["n", j], kept["z_bank", j][:].bitcast(BF16)
             for cols in column_parts(j):
                 nc.vector.scalar_tensor_tensor(
-                    out=n[:, cols], in0=z_sb[j][:, cols], scalar=1.0, in1=n[:, cols], op0=ALU.subtract, op1=ALU.mult
+                    out=n[:, cols], in0=z_bank[:, cols], scalar=1.0, in1=n[:, cols], op0=ALU.subtract, op1=ALU.mult
                 )
 
         def blend(j, engine, cols):
@@ -292,8 +306,8 @@ def tile_layernormgrucell_pb_kernel(
         quantise(0, (HN,))
         transpose(0, (IN,))
         quantise(0, (IN,))
-        spread_bias(HN, gates, "r_bank", nc.scalar.copy)
-        spread_bias(IN, products, "acc", nc.vector.tensor_copy)
+        spread_bias(HN, ((gates, "r_bank"), (gates, "z_bank")), nc.scalar.copy)
+        spread_bias(IN, ((products, "acc"), (products, "acc")), nc.vector.tensor_copy)
         multiply(0)
         transpose(1)
         add_bias(0)
@@ -304,37 +318,48 @@ def tile_layernormgrucell_pb_kernel(
         transpose(2)
         inverse_std(0)
         keep_old(0)
-        pool_cols, vector_cols = slice(0, POOL_COLS), slice(POOL_COLS, H)
-        for i in range(1, ROW_TILES + 2):
+        pool_cols, vector_cols, all_cols = slice(0, POOL_COLS), slice(POOL_COLS, H), slice(0, H)
+        last = ROW_TILES - 1
+        for i in range(1, ROW_TILES):
+            keep_old(i)
             if live(i - 3):
                 blend(i - 3, nc.gpsimd, pool_cols)
-            if live(i):
-                keep_old(i)
-            if live(i - 1):
-                reset_gate(i - 1)
-                row_scalars(i - 1)
+            reset_gate(i - 1)
+            row_scalars(i - 1)
             if live(i + 2):
                 transpose(i + 2)
-            if live(i):
-                reset_to_psum(i)
-                add_bias(i)
+            turn_update(i - 1)
+            reset_to_psum(i)
+            add_bias(i)
+            if live(i - 2):
+                take_new(i - 2)
             if live(i + 1):
                 quantise(i + 1)
-            if live(i):
-                deviations(i)
+            deviations(i)
+            update_to_psum(i - 1)
+            add_input_path(i - 1)
+            candidate(i - 1)
             if live(i - 3):
                 blend(i - 3, nc.vector, vector_cols)
                 store(i - 3, pool_cols)
                 store(i - 3, vector_cols)
-            if live(i - 1):
-                add_input_path(i - 1)
-                candidate(i - 1)
-            if live(i - 2):
-                take_new(i - 2)
-            if live(i):
-                inverse_std(i)
+            inverse_std(i)
             if live(i + 1):
                 multiply(i + 1)
-        for cols in column_parts(ROW_TILES - 1):
-            blend(ROW_TILES - 1, nc.vector, cols)
-            store(ROW_TILES - 1, cols)
+        blend(last - 2, nc.gpsimd, pool_cols)
+        reset_gate(last)
+        row_scalars(last)
+        take_new(last - 1)
+        turn_update(last)
+        update_to_psum(last)
+        blend(last - 2, nc.vector, vector_cols)
+        store(last - 2, pool_cols)
+        store(last - 2, vector_cols)
+        add_input_path(last)
+        candidate(last)
+        blend(last - 1, nc.vector, all_cols)
+        store(last - 1, all_cols)
+        take_new(last)
+        for cols in column_parts(last):
+            blend(last, nc.vector, cols)
+            store(last, cols)

@@ -308,14 +308,15 @@ def tile_layernormgrucell_pb_kernel(
         quantise(0, (IN,))
         spread_bias(HN, ((gates, "r_bank"), (gates, "z_bank")), nc.scalar.copy)
         spread_bias(IN, ((products, "acc"), (products, "acc")), nc.vector.tensor_copy)
-        multiply(0)
+        multiply(0, (HN,))
         transpose(1)
+        multiply(0, (IN,))
         add_bias(0)
         quantise(1)
         deviations(0)
         reset_to_psum(0)
-        multiply(1)
         transpose(2)
+        multiply(1)
         inverse_std(0)
         keep_old(0)
         pool_cols, vector_cols, all_cols = slice(0, POOL_COLS), slice(POOL_COLS, H), slice(0, H)

@@ -24,7 +24,7 @@ HALVES = H // BANK
 WORD_BLOCKS = H * 2 // 4 // P
 EPS = 1e-5
 HN, IN = 0, 1
-POOL_COLS = 512
+POOL_COLS = 256
 LAST_PARTS = 2
 LEAD = 2
 
@@ -114,10 +114,7 @@ def tile_layernormgrucell_pb_kernel(
                 nc.tensor.matmul(out=spread[:], lhsT=ones[:], rhs=bias_rows[:, path, cols], start=True, stop=True)
                 copy(out=bias[:, path, cols], in_=spread[:])
 
-        def transpose(j, paths=(HN, IN)):
-            if paths[0] == HN:
-                kept["grouped", j] = stage.tile([P, 2, PASSES, P, PACK], BF16, align_bytes=64, name="grouped")
-            grouped = kept["grouped", j]
+        def turn(j, paths=(HN, IN)):
             for path in paths:
                 pairs = (h_sb, x_sb)[path][j][:].bitcast(F32)
                 turned = flipped.tile([P, PASSES, 2, P], F32, tag="turned")
@@ -126,9 +123,15 @@ def tile_layernormgrucell_pb_kernel(
                         nc.tensor.transpose(
                             turned[:, g, u, :], pairs[:, 256 * g + u : 256 * (g + 1) : 2], ident[:]
                         )
+                kept["turned", j, path] = turned
+
+        def group(j, paths=(HN, IN)):
+            if paths[0] == HN:
+                kept["grouped", j] = stage.tile([P, 2, PASSES, P, PACK], BF16, align_bytes=64, name="grouped")
+            for path in paths:
                 nc.scalar.copy(
-                    out=grouped[:, path].bitcast(F32),
-                    in_=turned[:].rearrange("p g u b -> p g b u"),
+                    out=kept["grouped", j][:, path].bitcast(F32),
+                    in_=kept["turned", j, path][:].rearrange("p g u b -> p g b u"),
                 )
 
         def quantise(j, paths=(HN, IN)):
@@ -177,31 +180,37 @@ def tile_layernormgrucell_pb_kernel(
             kept["u", j] = u
             kept["half_sums", j] = half_sums
 
-        def deviations(j):
-            u, half_sums = kept["u", j], kept["half_sums", j]
-            minus_mean = stats.tile([P, 2], F32)
-            square_sums = stats.tile([P, 2], F32)
-            for path in (HN, IN):
-                unread_pair = stats.tile([P, HALVES], F32)
-                nc.scalar.activation(
-                    out=unread_pair[:],
-                    in_=half_sums[:, path, :],
-                    func=ACT.Identity,
-                    scale=-1.0 / H,
-                    accum_out=minus_mean[:, path : path + 1],
-                )
-                unread = stage.tile([P, H], BF16)
-                nc.scalar.activation(
-                    out=unread[:],
-                    in_=u[:, path, :],
-                    func=ACT.Square,
-                    bias=minus_mean[:, path : path + 1],
-                    scale=1.0,
-                    accum_out=square_sums[:, path : path + 1],
-                )
+        def mean(j, path):
+            if path == HN:
+                kept["minus_mean", j] = stats.tile([P, 2], F32, name="minus_mean")
+            unread_pair = stats.tile([P, HALVES], F32)
+            nc.scalar.activation(
+                out=unread_pair[:],
+                in_=kept["half_sums", j][:, path, :],
+                func=ACT.Identity,
+                scale=-1.0 / H,
+                accum_out=kept["minus_mean", j][:, path : path + 1],
+            )
+
+        def squares(j, path):
+            if path == HN:
+                kept["square_sums", j] = stats.tile([P, 2], F32, name="square_sums")
+            unread = stage.tile([P, H], BF16)
+            nc.scalar.activation(
+                out=unread[:],
+                in_=kept["u", j][:, path, :],
+                func=ACT.Square,
+                bias=kept["minus_mean", j][:, path : path + 1],
+                scale=1.0,
+                accum_out=kept["square_sums", j][:, path : path + 1],
+            )
+
+        def variances(j):
             var_eps = stats.tile([P, 2], F32)
-            nc.scalar.activation(out=var_eps[:], in_=square_sums[:], func=ACT.Identity, bias=EPS, scale=1.0 / H)
-            kept["minus_mean", j], kept["var_eps", j] = minus_mean, var_eps
+            nc.scalar.activation(
+                out=var_eps[:], in_=kept["square_sums", j][:], func=ACT.Identity, bias=EPS, scale=1.0 / H
+            )
+            kept["var_eps", j] = var_eps
 
         def inverse_std(j):
             rstd = stats.tile([P, 2], F32)
@@ -242,8 +251,11 @@ def tile_layernormgrucell_pb_kernel(
             turned = flipped.tile([P, WORD_BLOCKS, P], F32, tag="turned")
             for c in range(WORD_BLOCKS):
                 nc.tensor.transpose(turned[:, c, :], words[:, P * c : P * (c + 1)], ident[:])
+            kept["turned_z", j] = turned
+
+        def update_from_psum(j):
             z_turned = stage.tile([P, WORD_BLOCKS, P], F32)
-            nc.scalar.copy(out=z_turned[:], in_=turned[:])
+            nc.scalar.copy(out=z_turned[:], in_=kept["turned_z", j][:])
             kept["z_turned", j] = z_turned
 
         def update_to_psum(j):
@@ -280,9 +292,9 @@ def tile_layernormgrucell_pb_kernel(
                 )
             kept["n", j] = n
 
-        def keep_old(j):
+        def keep_old(j, engine):
             old = blends.tile([P, H], F32)
-            nc.gpsimd.tensor_tensor(out=old[:], in0=z_sb[j][:], in1=h_sb[j][:], op=ALU.mult)
+            engine.tensor_tensor(out=old[:], in0=z_sb[j][:], in1=h_sb[j][:], op=ALU.mult)
             kept["old", j] = old
 
         def take_new(j):
@@ -302,33 +314,41 @@ def tile_layernormgrucell_pb_kernel(
         def live(j):
             return 0 <= j < ROW_TILES
 
-        transpose(0, (HN,))
+        turn(0, (HN,))
+        group(0, (HN,))
         quantise(0, (HN,))
-        transpose(0, (IN,))
+        turn(0, (IN,))
+        group(0, (IN,))
         quantise(0, (IN,))
         spread_bias(HN, ((gates, "r_bank"), (gates, "z_bank")), nc.scalar.copy)
         spread_bias(IN, ((products, "acc"), (products, "acc")), nc.vector.tensor_copy)
         multiply(0, (HN,))
-        transpose(1)
+        turn(1)
+        group(1)
         multiply(0, (IN,))
         add_bias(0)
         quantise(1)
-        deviations(0)
+        for path in (HN, IN):
+            mean(0, path)
+            squares(0, path)
+        variances(0)
         reset_to_psum(0)
-        transpose(2)
+        turn(2)
+        group(2)
         multiply(1)
         inverse_std(0)
-        keep_old(0)
         pool_cols, vector_cols, all_cols = slice(0, POOL_COLS), slice(POOL_COLS, H), slice(0, H)
         last = ROW_TILES - 1
         for i in range(1, ROW_TILES):
-            keep_old(i)
+            keep_old(i, nc.gpsimd)
             if live(i - 3):
                 blend(i - 3, nc.gpsimd, pool_cols)
             reset_gate(i - 1)
             row_scalars(i - 1)
             if live(i + 2):
-                transpose(i + 2)
+                turn(i + 2)
+            if live(i + 2):
+                group(i + 2)
             turn_update(i - 1)
             reset_to_psum(i)
             add_bias(i)
@@ -336,7 +356,14 @@ def tile_layernormgrucell_pb_kernel(
                 take_new(i - 2)
             if live(i + 1):
                 quantise(i + 1)
-            deviations(i)
+            if i == 1:
+                keep_old(0, nc.vector)
+            mean(i, HN)
+            update_from_psum(i - 1)
+            squares(i, HN)
+            mean(i, IN)
+            squares(i, IN)
+            variances(i)
             update_to_psum(i - 1)
             add_input_path(i - 1)
             candidate(i - 1)
@@ -352,6 +379,7 @@ def tile_layernormgrucell_pb_kernel(
         row_scalars(last)
         take_new(last - 1)
         turn_update(last)
+        update_from_psum(last)
         update_to_psum(last)
         blend(last - 2, nc.vector, vector_cols)
         store(last - 2, pool_cols)

@@ -24,7 +24,7 @@ HALVES = H // BANK
 WORD_BLOCKS = H * 2 // 4 // P
 EPS = 1e-5
 HN, IN = 0, 1
-POOL_COLS = 256
+POOL_COLS = 384
 LAST_PARTS = 2
 LEAD = 2
 
@@ -336,6 +336,7 @@ def tile_layernormgrucell_pb_kernel(
         turn(2)
         group(2)
         multiply(1)
+        turn(3)
         inverse_std(0)
         pool_cols, vector_cols, all_cols = slice(0, POOL_COLS), slice(POOL_COLS, H), slice(0, H)
         last = ROW_TILES - 1
@@ -344,13 +345,12 @@ def tile_layernormgrucell_pb_kernel(
             if live(i - 3):
                 blend(i - 3, nc.gpsimd, pool_cols)
             reset_gate(i - 1)
-            row_scalars(i - 1)
-            if live(i + 2):
-                turn(i + 2)
             if live(i + 2):
                 group(i + 2)
-            turn_update(i - 1)
             reset_to_psum(i)
+            turn_update(i - 1)
+            if live(i + 3):
+                turn(i + 3)
             add_bias(i)
             if live(i - 2):
                 take_new(i - 2)
@@ -359,9 +359,10 @@ def tile_layernormgrucell_pb_kernel(
             if i == 1:
                 keep_old(0, nc.vector)
             mean(i, HN)
-            update_from_psum(i - 1)
+            row_scalars(i - 1)
             squares(i, HN)
             mean(i, IN)
+            update_from_psum(i - 1)
             squares(i, IN)
             variances(i)
             update_to_psum(i - 1)

from contextlib import ExitStack

import concourse.mybir as mybir
from concourse.masks import make_identity

F32 = mybir.dt.float32
BF16 = mybir.dt.bfloat16
I32 = mybir.dt.int32
U32 = mybir.dt.uint32
U8 = mybir.dt.uint8
FP8X4 = mybir.dt.float8_e4m3fn_x4
FP4X4 = mybir.dt.float4_e2m1fn_x4
ALU = mybir.AluOpType
ACT = mybir.ActivationFunctionType

P = 128
PACK = 4
K_PASS = P * PACK
BATCH, K, H = 1024, 1024, 1024
ROW_TILES = BATCH // P
PASSES = K // K_PASS
BANK = 512
HALVES = H // BANK
WORD_BLOCKS = H * 2 // 4 // P
EPS = 1e-5
HN, IN = 0, 1
POOL_COLS = 384
LAST_PARTS = 2
LEAD = 2

FLOPS = 2 * 2 * BATCH * K * H


def tile_layernormgrucell_pb_kernel(
    tc, x, h, r, z, W_in_words, W_in_scales, b_in, W_hn_words, W_hn_scales, b_hn, out
):
    nc = tc.nc
    with ExitStack() as ctx:
        const = ctx.enter_context(tc.tile_pool(name="const", bufs=1))
        inputs = ctx.enter_context(tc.tile_pool(name="inputs", bufs=1))
        stage = ctx.enter_context(tc.tile_pool(name="stage", bufs=2))
        packed = ctx.enter_context(tc.tile_pool(name="packed", bufs=3))
        work = ctx.enter_context(tc.tile_pool(name="work", bufs=3))
        stats = ctx.enter_context(tc.tile_pool(name="stats", bufs=4))
        blends = ctx.enter_context(tc.tile_pool(name="blends", bufs=4))
        flipped = ctx.enter_context(tc.psum_pool(name="flipped", bufs=2))
        gates = ctx.enter_context(tc.psum_pool(name="gates", bufs=1))
        products = ctx.enter_context(tc.psum_pool(name="products", bufs=4))
        ctx.enter_context(tc.manual_schedule())

        w_words, w_plane = [], []
        bias_rows = const.tile([P, 2, H], BF16)
        for path in (HN, IN):
            w_words.append(const.tile([P, PASSES, 2 * H], U8, name="w_words%d" % path, align_bytes=64))
            w_plane.append(const.tile([P, PASSES, H], U8, name="w_plane%d" % path, align_bytes=64))
        nc.vector.memset(w_plane[HN][:].bitcast(I32), 0)
        nc.vector.memset(bias_rows[:].bitcast(I32), 0)
        nc.vector.memset(w_plane[IN][:].bitcast(I32), 0)
        ident = const.tile([P, P], F32)
        make_identity(nc, ident[:])
        ident_bf = const.tile([P, P], BF16)
        make_identity(nc, ident_bf[:])
        ones = const.tile([P, P], BF16)
        nc.gpsimd.memset(ones[:], 1.0)
        minus_half = const.tile([P, 2], F32)
        nc.gpsimd.memset(minus_half[:], -0.5)
        bias = const.tile([P, 2, H], BF16)

        h_sb, x_sb, r_sb, z_sb = [], [], [], []

        def load_rows(loaded, src, label):
            j = len(loaded)
            rows = inputs.tile([P, K], BF16, name="%s%d" % (label, j))
            nc.sync.dma_start(out=rows[:], in_=src[j * P : (j + 1) * P, :])
            loaded.append(rows)

        def load_scales(path, scales):
            for quad in range(4):
                nc.sync.dma_start(
                    out=w_plane[path][32 * quad : 32 * quad + 4, :, :].bitcast(I32),
                    in_=scales[:, 4 * quad : 4 * quad + 4, :].bitcast(I32).rearrange("g q n -> q g n"),
                )

        def load_words(path, words):
            nc.sync.dma_start(
                out=w_words[path][:].bitcast(I32),
                in_=words.bitcast(I32).rearrange("g p c -> p g c"),
            )

        load_rows(h_sb, h, "h")
        load_rows(x_sb, x, "x")
        load_scales(HN, W_hn_scales)
        nc.sync.dma_start(out=bias_rows[0:1, HN, :], in_=b_hn.rearrange("(o n) -> o n", o=1))
        nc.sync.dma_start(out=bias_rows[0:1, IN, :], in_=b_in.rearrange("(o n) -> o n", o=1))
        load_words(HN, W_hn_words)
        load_scales(IN, W_in_scales)
        load_words(IN, W_in_words)
        for j in range(ROW_TILES):
            for ahead in range(LEAD if j == 0 else 1):
                if len(h_sb) < ROW_TILES:
                    load_rows(h_sb, h, "h")
                    load_rows(x_sb, x, "x")
                if ahead == 0:
                    load_rows(r_sb, r, "r")
            load_rows(z_sb, z, "z")

        kept = {}

        def spread_bias(path, banks, copy):
            for half in range(HALVES):
                cols = slice(BANK * half, BANK * (half + 1))
                pool, tag = banks[half]
                spread = pool.tile([P, BANK], F32, tag=tag)
                nc.tensor.matmul(out=spread[:], lhsT=ones[:], rhs=bias_rows[:, path, cols], start=True, stop=True)
                copy(out=bias[:, path, cols], in_=spread[:])

        def turn(j, paths=(HN, IN)):
            for path in paths:
                pairs = (h_sb, x_sb)[path][j][:].bitcast(F32)
                turned = flipped.tile([P, PASSES, 2, P], F32, tag="turned")
                for g in range(PASSES):
                    for u in range(2):
                        nc.tensor.transpose(
                            turned[:, g, u, :], pairs[:, 256 * g + u : 256 * (g + 1) : 2], ident[:]
                        )
                kept["turned", j, path] = turned

        def group(j, paths=(HN, IN)):
            if paths[0] == HN:
                kept["grouped", j] = stage.tile([P, 2, PASSES, P, PACK], BF16, align_bytes=64, name="grouped")
            for path in paths:
                nc.scalar.copy(
                    out=kept["grouped", j][:, path].bitcast(F32),
                    in_=kept["turned", j, path][:].rearrange("p g u b -> p g b u"),
                )

        def quantise(j, paths=(HN, IN)):
            if paths[0] == HN:
                kept["codes", j] = packed.tile([P, 2, PASSES, P], U32, align_bytes=64, name="codes")
                kept["plane", j] = packed.tile([P, 2, PASSES, P], U8, align_bytes=64, name="plane")
            some = slice(paths[0], paths[-1] + 1)
            nc.vector.quantize_mx(
                out=kept["codes", j][:, some].rearrange("p a g b -> p (a g b)").bitcast(FP8X4),
                scales=kept["plane", j][:, some].rearrange("p a g b -> p (a g b)"),
                in_=kept["grouped", j][:, some].rearrange("p a g b t -> p (a g b t)"),
            )

        def multiply(j, paths=(HN, IN)):
            codes, plane = kept["codes", j], kept["plane", j]
            for path in paths:
                for half in range(HALVES):
                    acc = products.tile([P, BANK], F32, tag="acc")
                    for g in range(PASSES):
                        nc.tensor.matmul_mx(
                            out=acc[:],
                            lhsT=codes[:, path, g, :].bitcast(FP8X4),
                            lhsT_scale=plane[:, path, g, :],
                            rhs=w_words[path][:, g, 2 * BANK * half : 2 * BANK * (half + 1)].bitcast(FP4X4),
                            rhs_scale=w_plane[path][:, g, BANK * half : BANK * (half + 1)],
                            start=(g == 0),
                            stop=(g == PASSES - 1),
                        )
                    kept["acc", j, path, half] = acc

        def add_bias(j):
            u = work.tile([P, 2, H], F32)
            half_sums = stats.tile([P, 2, HALVES], F32)
            for path in (HN, IN):
                for half in range(HALVES):
                    cols = slice(BANK * half, BANK * (half + 1))
                    nc.vector.scalar_tensor_tensor(
                        out=u[:, path, cols],
                        in0=kept["acc", j, path, half][:],
                        scalar=1.0,
                        in1=bias[:, path, cols],
                        op0=ALU.mult,
                        op1=ALU.add,
                        accum_out=half_sums[:, path, half : half + 1],
                    )
            kept["u", j] = u
            kept["half_sums", j] = half_sums

        def mean(j, path):
            if path == HN:
                kept["minus_mean", j] = stats.tile([P, 2], F32, name="minus_mean")
            unread_pair = stats.tile([P, HALVES], F32)
            nc.scalar.activation(
                out=unread_pair[:],
                in_=kept["half_sums", j][:, path, :],
                func=ACT.Identity,
                scale=-1.0 / H,
                accum_out=kept["minus_mean", j][:, path : path + 1],
            )

        def squares(j, path):
            if path == HN:
                kept["square_sums", j] = stats.tile([P, 2], F32, name="square_sums")
            unread = stage.tile([P, H], BF16)
            nc.scalar.activation(
                out=unread[:],
                in_=kept["u", j][:, path, :],
                func=ACT.Square,
                bias=kept["minus_mean", j][:, path : path + 1],
                scale=1.0,
                accum_out=kept["square_sums", j][:, path : path + 1],
            )

        def variances(j):
            var_eps = stats.tile([P, 2], F32)
            nc.scalar.activation(
                out=var_eps[:], in_=kept["square_sums", j][:], func=ACT.Identity, bias=EPS, scale=1.0 / H
            )
            kept["var_eps", j] = var_eps

        def inverse_std(j):
            rstd = stats.tile([P, 2], F32)
            nc.gpsimd.tensor_tensor(out=rstd[:], in0=kept["var_eps", j][:], in1=minus_half[:], op=ALU.pow)
            kept["rstd", j] = rstd

        def row_scalars(j):
            rstd_h, rstd_i = kept["rstd", j][:, HN : HN + 1], kept["rstd", j][:, IN : IN + 1]
            std_i = stats.tile([P, 1], F32)
            nc.scalar.activation(out=std_i[:], in_=kept["var_eps", j][:, IN : IN + 1], func=ACT.Copy, scale=rstd_i)
            shift = stats.tile([P, 1], F32)
            nc.scalar.activation(out=shift[:], in_=kept["minus_mean", j][:, IN : IN + 1], func=ACT.Copy, scale=rstd_i)
            ratio = stats.tile([P, 1], F32)
            nc.scalar.activation(out=ratio[:], in_=std_i[:], func=ACT.Copy, scale=rstd_h)
            kept["ratio", j], kept["shift", j] = ratio, shift

        def reset_to_psum(j):
            r_bank = gates.tile([P, H], BF16, tag="r_bank")
            for half in range(HALVES):
                cols = slice(BANK * half, BANK * (half + 1))
                nc.tensor.matmul(out=r_bank[:, cols], lhsT=ident_bf[:], rhs=r_sb[j][:, cols], start=True, stop=True)
            kept["r_bank", j] = r_bank

        def reset_gate(j):
            gated = work.tile([P, H], F32)
            nc.vector.scalar_tensor_tensor(
                out=gated[:],
                in0=kept["u", j][:, HN, :],
                scalar=kept["minus_mean", j][:, HN : HN + 1],
                in1=kept["r_bank", j][:],
                op0=ALU.add,
                op1=ALU.mult,
            )
            kept["gated", j] = gated

        def turn_update(j):
            words = z_sb[j][:].bitcast(F32)
            turned = flipped.tile([P, WORD_BLOCKS, P], F32, tag="turned")
            for c in range(WORD_BLOCKS):
                nc.tensor.transpose(turned[:, c, :], words[:, P * c : P * (c + 1)], ident[:])
            kept["turned_z", j] = turned

        def update_from_psum(j):
            z_turned = stage.tile([P, WORD_BLOCKS, P], F32)
            nc.scalar.copy(out=z_turned[:], in_=kept["turned_z", j][:])
            kept["z_turned", j] = z_turned

        def update_to_psum(j):
            z_bank = gates.tile([P, WORD_BLOCKS * P], F32, tag="z_bank")
            for c in range(WORD_BLOCKS):
                nc.tensor.transpose(z_bank[:, P * c : P * (c + 1)], kept["z_turned", j][:, c, :], ident[:])
            kept["z_bank", j] = z_bank

        def column_parts(j):
            parts = LAST_PARTS if j == ROW_TILES - 1 else 1
            return [slice(c * H // parts, (c + 1) * H // parts) for c in range(parts)]

        def add_input_path(j):
            gated = kept["gated", j]
            for cols in column_parts(j):
                nc.vector.scalar_tensor_tensor(
                    out=gated[:, cols],
                    in0=gated[:, cols],
                    scalar=kept["ratio", j][:],
                    in1=kept["u", j][:, IN, cols],
                    op0=ALU.mult,
                    op1=ALU.add,
                )

        def candidate(j):
            n = blends.tile([P, H], F32)
            for cols in column_parts(j):
                nc.scalar.activation(
                    out=n[:, cols],
                    in_=kept["gated", j][:, cols],
                    func=ACT.Tanh,
                    bias=kept["shift", j][:],
                    scale=kept["rstd", j][:, IN : IN + 1],
                )
            kept["n", j] = n

        def keep_old(j, engine):
            old = blends.tile([P, H], F32)
            engine.tensor_tensor(out=old[:], in0=z_sb[j][:], in1=h_sb[j][:], op=ALU.mult)
            kept["old", j] = old

        def take_new(j):
            n, z_bank = kept["n", j], kept["z_bank", j][:].bitcast(BF16)
            for cols in column_parts(j):
                nc.vector.scalar_tensor_tensor(
                    out=n[:, cols], in0=z_bank[:, cols], scalar=1.0, in1=n[:, cols], op0=ALU.subtract, op1=ALU.mult
                )

        def blend(j, engine, cols):
            old, n = kept["old", j], kept["n", j]
            engine.tensor_tensor(out=n[:, cols], in0=old[:, cols], in1=n[:, cols], op=ALU.subtract)

        def store(j, cols):
            nc.sync.dma_start(out=out[j * P : (j + 1) * P, cols], in_=kept["n", j][:, cols])

        def live(j):
            return 0 <= j < ROW_TILES

        turn(0, (HN,))
        group(0, (HN,))
        quantise(0, (HN,))
        turn(0, (IN,))
        group(0, (IN,))
        quantise(0, (IN,))
        spread_bias(HN, ((gates, "r_bank"), (gates, "z_bank")), nc.scalar.copy)
        spread_bias(IN, ((products, "acc"), (products, "acc")), nc.vector.tensor_copy)
        multiply(0, (HN,))
        turn(1)
        group(1)
        multiply(0, (IN,))
        add_bias(0)
        quantise(1)
        for path in (HN, IN):
            mean(0, path)
            squares(0, path)
        variances(0)
        reset_to_psum(0)
        turn(2)
        group(2)
        multiply(1)
        turn(3)
        inverse_std(0)
        pool_cols, vector_cols, all_cols = slice(0, POOL_COLS), slice(POOL_COLS, H), slice(0, H)
        last = ROW_TILES - 1
        for i in range(1, ROW_TILES):
            keep_old(i, nc.gpsimd)
            if live(i - 3):
                blend(i - 3, nc.gpsimd, pool_cols)
            reset_gate(i - 1)
            if live(i + 2):
                group(i + 2)
            reset_to_psum(i)
            turn_update(i - 1)
            if live(i + 3):
                turn(i + 3)
            add_bias(i)
            if live(i - 2):
                take_new(i - 2)
            if live(i + 1):
                quantise(i + 1)
            if i == 1:
                keep_old(0, nc.vector)
            mean(i, HN)
            row_scalars(i - 1)
            squares(i, HN)
            mean(i, IN)
            update_from_psum(i - 1)
            squares(i, IN)
            variances(i)
            update_to_psum(i - 1)
            add_input_path(i - 1)
            candidate(i - 1)
            if live(i - 3):
                blend(i - 3, nc.vector, vector_cols)
                store(i - 3, pool_cols)
                store(i - 3, vector_cols)
            inverse_std(i)
            if live(i + 1):
                multiply(i + 1)
        blend(last - 2, nc.gpsimd, pool_cols)
        reset_gate(last)
        row_scalars(last)
        take_new(last - 1)
        turn_update(last)
        update_from_psum(last)
        update_to_psum(last)
        blend(last - 2, nc.vector, vector_cols)
        store(last - 2, pool_cols)
        store(last - 2, vector_cols)
        add_input_path(last)
        candidate(last)
        blend(last - 1, nc.vector, all_cols)
        store(last - 1, all_cols)
        take_new(last)
        for cols in column_parts(last):
            blend(last, nc.vector, cols)
            store(last, cols)
